import numpy as np
import ml_dtypes


BF16 = ml_dtypes.bfloat16


def bf(x):
    return np.asarray(x, np.float32).astype(BF16)


def f64(x):
    return np.asarray(x).astype(np.float64)


E2M1 = np.array([0.0, 0.5, 1.0, 1.5, 2.0, 3.0, 4.0, 6.0, -0.0, -0.5, -1.0, -1.5, -2.0, -3.0, -4.0, -6.0])


def pack_weight(w, fmt):
    k, n = w.shape
    w = f64(bf(w)).reshape(k // 32, 32, n)
    amax = np.abs(w).max(1)
    if fmt == "e4m3":
        byte = np.frexp(amax)[1] - 1 + 127 - 7
    else:
        mant, ex = np.frexp(amax / 6.0)
        byte = np.where(mant > 0.5, ex, ex - 1) + 127
    byte = np.clip(np.where(amax > 0, byte, 1), 1, 254)
    scaled = (w * np.exp2(127.0 - byte)[:, None, :]).reshape(k, n).astype(np.float32)
    by_word = np.ascontiguousarray(scaled.reshape(k // 512, 128, 4, n).transpose(0, 1, 3, 2))
    if fmt == "e4m3":
        words = by_word.astype(ml_dtypes.float8_e4m3fn).view(np.uint8)
    else:
        c = by_word.astype(ml_dtypes.float4_e2m1fn).view(np.uint8) & 0xF
        words = c[..., 0::2] | (c[..., 1::2] << 4)
    return np.ascontiguousarray(words), np.ascontiguousarray(byte.astype(np.uint8).reshape(k // 512, 16, n))


def unpack_weight(words, scales, fmt):
    g, p, n, _ = words.shape
    if fmt == "e4m3":
        vals = np.ascontiguousarray(words).view(ml_dtypes.float8_e4m3fn).astype(np.float64)
    else:
        nib = np.empty((g, p, n, 4), np.uint8)
        nib[..., 0::2] = words & 0xF
        nib[..., 1::2] = words >> 4
        vals = E2M1[nib]
    vals = vals * np.repeat(np.exp2(scales.astype(np.float64) - 127.0), 8, axis=1)[..., None]
    return vals.transpose(0, 1, 3, 2).reshape(g * 512, n)

def pack4(w):
    words, scales = pack_weight(w, "e2m1")
    return words.reshape(words.shape[0], 128, -1), scales


def unpack4(words, scales):
    return unpack_weight(words.reshape(words.shape[0], 128, -1, 2), scales, "e2m1")


def kspread(k):
    return np.exp2(np.repeat(np.random.randint(-6, 7, k // 32), 32).astype(np.float64))


B, L, D, H, HD, MINI, NCH, TEXT, OFF = 2, 256, 4096, 16, 256, 64, 4, 64, 128


def rope_table():
    inv_freq = 1.0 / (10000.0 ** (np.arange(0, HD, 2) / HD))
    ang = np.outer(np.arange(L), inv_freq)
    return np.stack([np.cos(ang), np.sin(ang)], axis=-1)


def l2norm(x):
    return x / np.maximum(np.sqrt((x * x).sum(-1, keepdims=True)), 1e-12)


def rope(x, cos, sin):
    c = cos[None, :, None, :]
    s = sin[None, :, None, :]
    xr, xi = x[..., 0::2], x[..., 1::2]
    return np.stack([xr * c - xi * s, xr * s + xi * c], axis=-1).reshape(x.shape)


def setup_inputs():
    s = kspread(D)
    hidden_states = np.random.standard_normal((B, L, D)) * s
    hidden_states_words, hidden_states_scales = pack4(hidden_states.reshape(B * L, D).T)
    freqs_cis = bf(rope_table())
    wq_words, wq_scales = pack4(np.random.standard_normal((D, D)) / np.sqrt(D) / s[:, None])
    wq_b = bf(np.random.standard_normal(D) * 0.1)
    wu_words, wu_scales = pack4(np.random.standard_normal((D, D)) / np.sqrt(D) / s[:, None])
    wu_b = bf(np.random.standard_normal(D) * 0.1)
    return {"hidden_states_words": hidden_states_words,
            "hidden_states_scales": hidden_states_scales,
            "freqs_cis": freqs_cis,
            "wq_w_words": wq_words,
            "wq_w_scales": wq_scales,
            "wq_b": wq_b,
            "wu_w_words": wu_words,
            "wu_w_scales": wu_scales,
            "wu_b": wu_b}


def reference(hidden_states_words, hidden_states_scales, freqs_cis, wq_w_words, wq_w_scales, wq_b, wu_w_words, wu_w_scales, wu_b):
    hq = unpack4(hidden_states_words, hidden_states_scales).T.reshape(B, L, D)
    xq = ((hq @ unpack4(wq_w_words, wq_w_scales)) + f64(wq_b)).reshape(B, L, H, HD)
    xu = ((hq @ unpack4(wu_w_words, wu_w_scales)) + f64(wu_b)).reshape(B, L, H, HD)
    fc = f64(freqs_cis)
    cos, sin = fc[..., 0], fc[..., 1]
    return rope(l2norm(xq), cos, sin), rope(l2norm(xu), cos, sin)

@@ -1,0 +1,289 @@
+from contextlib import ExitStack
+
+import concourse.mybir as mybir
+
+F32 = mybir.dt.float32
+BF16 = mybir.dt.bfloat16
+I32 = mybir.dt.int32
+U8 = mybir.dt.uint8
+FP4X4 = mybir.dt.float4_e2m1fn_x4
+ADD = mybir.AluOpType.add
+MULT = mybir.AluOpType.mult
+MAX = mybir.AluOpType.max
+ACT = mybir.ActivationFunctionType
+
+P = 128
+TOK = 512
+D = 4096
+HD = 256
+G = D // 512
+MT = TOK // P
+W = 1024
+NB = D // W
+HPB = W // HD
+RING = 3
+
+FLOPS = 2 * TOK * D * (2 * D)
+
+
+def tile_tttwrapper_pb_kernel(
+    tc, x_words, x_scales, freqs, wq_words, wq_scales, wq_b, wu_words, wu_scales, wu_b, out_q, out_u
+):
+    nc = tc.nc
+    streams = [
+        (wq_words, wq_scales, wq_b, out_q.rearrange("b l h f -> (b l) (h f)")),
+        (wu_words, wu_scales, wu_b, out_u.rearrange("b l h f -> (b l) (h f)")),
+    ]
+
+    with ExitStack() as ctx:
+        keep = ctx.enter_context(tc.tile_pool(name="keep", bufs=1))
+        work = ctx.enter_context(tc.tile_pool(name="work", bufs=2))
+        psum = ctx.enter_context(tc.psum_pool(name="psum", bufs=8))
+        ctx.enter_context(tc.manual_schedule())
+
+        xc = keep.tile([P, G, 2 * TOK], U8, align_bytes=256, name="xc")
+        xs = keep.tile([P, G, TOK], U8, align_bytes=256, name="xs")
+        half_c = []
+        half_s = []
+        for h in range(2):
+            hc = keep.tile([P, G, W], U8, align_bytes=256, name="hc%d" % h)
+            hs = keep.tile([P, G, W // 2], U8, align_bytes=256, name="hs%d" % h)
+            half_c.append(hc)
+            half_s.append(hs)
+        ring_c = []
+        ring_s = []
+        for r in range(RING):
+            rc = keep.tile([P, G, 2 * W], U8, align_bytes=256, name="rc%d" % r)
+            rs = keep.tile([P, G, W], U8, align_bytes=256, name="rs%d" % r)
+            ring_c.append(rc)
+            ring_s.append(rs)
+        cos_t = keep.tile([P, 2, HD], F32, name="cos_t")
+        sin_t = keep.tile([P, 2, HD], F32, name="sin_t")
+        fr = keep.tile([P, 2, HD], BF16, name="fr")
+        ones = keep.tile([P, P], BF16, name="ones")
+        brow = keep.tile([P, W], BF16, name="brow")
+        bias0 = keep.tile([P, W], F32, name="bias0")
+        bias_q = keep.tile([P, D - W], BF16, name="bias_q")
+        bias_u = keep.tile([P, D], BF16, name="bias_u")
+
+        def load_scales(dst, src, c0, width):
+            for q in range(4):
+                nc.sync.dma_start(
+                    out=dst[32 * q : 32 * q + 4, :, :].bitcast(I32),
+                    in_=src[:, 4 * q : 4 * q + 4, c0 : c0 + width].rearrange("g r n -> r g n").bitcast(I32),
+                )
+
+        def load_codes(dst, src, g0, g1, c0, width):
+            nc.sync.dma_start(
+                out=dst[:, g0:g1, :].bitcast(I32),
+                in_=src[g0:g1, :, 2 * c0 : 2 * (c0 + width)].rearrange("g p n -> p g n").bitcast(I32),
+            )
+
+        nc.vector.memset(xs[:].rearrange("p g n -> p (g n)").bitcast(I32), 0)
+        nc.gpsimd.memset(brow[:], 0.0)
+        nc.gpsimd.dma_start(out=brow[0:1, :], in_=wq_b[0:W].unsqueeze(0))
+        nc.gpsimd.dma_start(out=fr[:], in_=freqs.rearrange("(t p) j c -> p t (j c)", p=P))
+        nc.gpsimd.memset(ones[:], 1.0)
+        nc.vector.memset(half_s[0][:].rearrange("p g n -> p (g n)").bitcast(I32), 0)
+        nc.vector.memset(half_s[1][:].rearrange("p g n -> p (g n)").bitcast(I32), 0)
+        nc.vector.memset(ring_s[0][:].rearrange("p g n -> p (g n)").bitcast(I32), 0)
+        for r in range(1, RING):
+            nc.gpsimd.memset(ring_s[r][:].rearrange("p g n -> p (g n)").bitcast(I32), 0)
+
+        load_codes(xc, x_words, 0, 1, 0, TOK)
+        load_codes(half_c[0], wq_words, 0, 1, 0, W // 2)
+        load_scales(xs, x_scales, 0, TOK)
+        load_scales(half_s[0], wq_scales, 0, W // 2)
+        load_codes(xc, x_words, 1, 4, 0, TOK)
+        load_codes(half_c[0], wq_words, 1, 4, 0, W // 2)
+        load_codes(xc, x_words, 4, 8, 0, TOK)
+        load_codes(half_c[0], wq_words, 4, 8, 0, W // 2)
+        load_codes(half_c[1], wq_words, 0, 8, W // 2, W // 2)
+        load_scales(half_s[1], wq_scales, W // 2, W // 2)
+
+        def load_block(s):
+            words, scales, _, _ = streams[s // NB]
+            c0 = (s % NB) * W
+            r = (s - 1) % RING
+            load_codes(ring_c[r], words, 0, G, c0, W)
+            load_scales(ring_s[r], scales, c0, W)
+
+        for s in range(1, 1 + RING):
+            load_block(s)
+
+        for h in range(2):
+            bank = psum.tile([P, W // 2], F32, name="bank")
+            nc.tensor.matmul(
+                out=bank[:], lhsT=ones[:], rhs=brow[:, h * (W // 2) : (h + 1) * (W // 2)], start=True, stop=True
+            )
+            nc.scalar.copy(out=bias0[:, h * (W // 2) : (h + 1) * (W // 2)], in_=bank[:])
+
+        frv = fr[:].rearrange("p t (j c) -> p t j c", c=2)
+        cv = cos_t[:].rearrange("p t (j c) -> p t j c", c=2)
+        sv = sin_t[:].rearrange("p t (j c) -> p t j c", c=2)
+        nc.vector.tensor_copy(out=cv[:, :, :, 0], in_=frv[:, :, :, 0])
+        nc.vector.tensor_copy(out=cv[:, :, :, 1], in_=frv[:, :, :, 0])
+        nc.vector.tensor_scalar_mul(out=sv[:, :, :, 0], in0=frv[:, :, :, 1], scalar1=-1.0)
+        nc.vector.tensor_copy(out=sv[:, :, :, 1], in_=frv[:, :, :, 1])
+
+        def weights(s, c, w, g):
+            if s == 0:
+                h, c = divmod(c, W // 2)
+                return half_c[h][:, g, 2 * c : 2 * (c + w)], half_s[h][:, g, c : c + w]
+            r = (s - 1) % RING
+            return ring_c[r][:, g, 2 * c : 2 * (c + w)], ring_s[r][:, g, c : c + w]
+
+        banks = {}
+
+        def matmuls(s, members):
+            for m, c, w in members:
+                bank = psum.tile([P, W // 2], F32, name="bank")
+                banks[(s, m, c)] = bank
+            for g in range(G):
+                for m, c, w in members:
+                    wc, ws = weights(s, c, w, g)
+                    nc.tensor.matmul_mx(
+                        out=banks[(s, m, c)][:, :w],
+                        lhsT=xc[:, g, 2 * P * m : 2 * P * (m + 1)].bitcast(FP4X4),
+                        lhsT_scale=xs[:, g, P * m : P * (m + 1)],
+                        rhs=wc.bitcast(FP4X4),
+                        rhs_scale=ws,
+                        start=(g == 0),
+                        stop=(g == G - 1),
+                    )
+
+        def bias_of(s):
+            if s == 0:
+                return bias0[:]
+            if s < NB:
+                return bias_q[:, (s - 1) * W : s * W]
+            return bias_u[:, (s - NB) * W : (s - NB + 1) * W]
+
+        state = {}
+
+        def front(i):
+            s, m, c0, groups = units[i]
+            w = sum(groups)
+            y = work.tile([P, W], F32, name="y")
+            b = bias_of(s)
+            at = 0
+            for gw in groups:
+                nc.vector.tensor_tensor(
+                    out=y[:, at : at + gw],
+                    in0=banks[(s, m, c0 + at)][:, :gw],
+                    in1=b[:, c0 + at : c0 + at + gw],
+                    op=ADD,
+                )
+                at += gw
+            ss = work.tile([P, HPB], F32, name="ss", bufs=4)
+            for j in range(w // HD):
+                junk = work.tile([P, HD], F32, name="junk")
+                nc.scalar.activation(
+                    out=junk[:], in_=y[:, j * HD : (j + 1) * HD], func=ACT.Square, accum_out=ss[:, j : j + 1]
+                )
+            state[i] = (y, ss)
+
+        def rotate(i):
+            s, m, c0, groups = units[i]
+            w = sum(groups)
+            n = w // HD
+            y, ss = state[i]
+            lt = m % 2
+            t1 = work.tile([P, W], F32, name="t1")
+            t2 = work.tile([P, W], F32, name="t2")
+            nc.vector.tensor_tensor(
+                out=t1[:, :w].rearrange("p (h f) -> p h f", h=n),
+                in0=y[:, :w].rearrange("p (h f) -> p h f", h=n),
+                in1=cos_t[:, lt, :].unsqueeze(1).to_broadcast([P, n, HD]),
+                op=MULT,
+            )
+            nc.vector.tensor_tensor(
+                out=t2[:, :w].rearrange("p (h j c) -> p h j c", h=n, c=2),
+                in0=y[:, :w].rearrange("p (h j c) -> p h j c", h=n, c=2)[:, :, :, ::-1],
+                in1=sin_t[:, lt, :].rearrange("p (j c) -> p j c", c=2).unsqueeze(1).to_broadcast([P, n, HD // 2, 2]),
+                op=MULT,
+            )
+            ssm = work.tile([P, HPB], F32, name="ssm", bufs=4)
+            nc.gpsimd.tensor_scalar(out=ssm[:, :n], in0=ss[:, :n], scalar1=1e-24, scalar2=None, op0=MAX)
+            state[i] = (t1, t2, ssm)
+
+        def shared(i):
+            w = sum(units[i][3])
+            return w // 2 if w >= W // 2 else 0
+
+        def add_g(i):
+            t1, t2, ssm = state[i]
+            u = work.tile([P, W], F32, name="u", bufs=3)
+            k = shared(i)
+            if k:
+                nc.gpsimd.tensor_tensor(out=u[:, :k], in0=t1[:, :k], in1=t2[:, :k], op=ADD)
+            state[i] = (t1, t2, ssm, u)
+
+        def add_v(i):
+            t1, t2, ssm, u = state[i]
+            k = shared(i)
+            w = sum(units[i][3])
+            nc.vector.tensor_tensor(out=u[:, k:w], in0=t1[:, k:w], in1=t2[:, k:w], op=ADD)
+
+        def finish(i):
+            t1, t2, ssm, u = state[i]
+            s, m, c0, groups = units[i]
+            w = sum(groups)
+            n = w // HD
+            inv = work.tile([P, HPB], F32, name="inv", bufs=4)
+            nc.scalar.activation(out=inv[:, :n], in_=ssm[:, :n], func=ACT.Abs_reciprocal_sqrt)
+            o = work.tile([P, W], F32, name="o", bufs=4)
+            for j in range(n):
+                nc.scalar.activation(
+                    out=o[:, j * HD : (j + 1) * HD],
+                    in_=u[:, j * HD : (j + 1) * HD],
+                    func=ACT.Copy,
+                    scale=inv[:, j : j + 1],
+                )
+            dst = streams[s // NB][3]
+            col = (s % NB) * W + c0
+            nc.sync.dma_start(out=dst[m * P : (m + 1) * P, col : col + w], in_=o[:, :w])
+
+        units = []
+        for s in range(2 * NB):
+            for m in range(MT):
+                left = (2 * NB - s) * MT - m
+                if left > 4:
+                    units.append((s, m, 0, [512, 512]))
+                elif left > 1:
+                    units.append((s, m, 0, [512]))
+                    units.append((s, m, 512, [512]))
+                else:
+                    units.append((s, m, 0, [512]))
+                    units.append((s, m, 512, [256]))
+                    units.append((s, m, 768, [256]))
+
+        for i in range(len(units)):
+            s, m, c0, groups = units[i]
+            if i == 0:
+                matmuls(0, [(0, 0, 512), (1, 0, 512)])
+                matmuls(0, [(0, 512, 512)])
+                matmuls(0, [(1, 512, 512)])
+            elif i > 1:
+                at = c0
+                for gw in groups:
+                    matmuls(s, [(m, at, gw)])
+                    at += gw
+            if i > 0:
+                add_g(i - 1)
+            front(i)
+            if i > 0:
+                add_v(i - 1)
+            rotate(i)
+            if i > 0:
+                finish(i - 1)
+            if i == 0:
+                nc.gpsimd.dma_start(out=bias_q[:], in_=wq_b[W:D].partition_broadcast(P))
+            if i == 5:
+                nc.gpsimd.dma_start(out=bias_u[:], in_=wu_b.partition_broadcast(P))
+            if m == 0 and c0 == 0 and s >= 2 and s + RING - 1 < 2 * NB:
+                load_block(s + RING - 1)
+        last = len(units) - 1
+        add_g(last)
+        add_v(last)
+        finish(last)

@@ -63,14 +63,16 @@ def tile_tttwrapper_pb_kernel(
         ones = keep.tile([P, P], BF16, name="ones")
         brow = keep.tile([P, W], BF16, name="brow")
         bias0 = keep.tile([P, W], F32, name="bias0")
-        bias_q = keep.tile([P, D - W], BF16, name="bias_q")
-        bias_u = keep.tile([P, D], BF16, name="bias_u")
+        ring_b = []
+        for r in range(RING):
+            rb = keep.tile([P, W], BF16, name="rb%d" % r)
+            ring_b.append(rb)
 
         def load_scales(dst, src, c0, width):
-            for q in range(4):
+            for r in range(4):
                 nc.sync.dma_start(
-                    out=dst[32 * q : 32 * q + 4, :, :].bitcast(I32),
-                    in_=src[:, 4 * q : 4 * q + 4, c0 : c0 + width].rearrange("g r n -> r g n").bitcast(I32),
+                    out=dst[r:P:32, :, :].bitcast(I32),
+                    in_=src[:, r:16:4, c0 : c0 + width].rearrange("g q n -> q g n").bitcast(I32),
                 )
 
         def load_codes(dst, src, g0, g1, c0, width):
@@ -102,11 +104,12 @@ def tile_tttwrapper_pb_kernel(
         load_scales(half_s[1], wq_scales, W // 2, W // 2)
 
         def load_block(s):
-            words, scales, _, _ = streams[s // NB]
+            words, scales, bias, dst = streams[s // NB]
             c0 = (s % NB) * W
             r = (s - 1) % RING
             load_codes(ring_c[r], words, 0, G, c0, W)
             load_scales(ring_s[r], scales, c0, W)
+            nc.sync.dma_start(out=ring_b[r][:], in_=bias[c0 : c0 + W].partition_broadcast(P))
 
         for s in range(1, 1 + RING):
             load_block(s)
@@ -155,9 +158,7 @@ def tile_tttwrapper_pb_kernel(
         def bias_of(s):
             if s == 0:
                 return bias0[:]
-            if s < NB:
-                return bias_q[:, (s - 1) * W : s * W]
-            return bias_u[:, (s - NB) * W : (s - NB + 1) * W]
+            return ring_b[(s - 1) % RING][:]
 
         state = {}
 
@@ -197,19 +198,23 @@ def tile_tttwrapper_pb_kernel(
                 in1=cos_t[:, lt, :].unsqueeze(1).to_broadcast([P, n, HD]),
                 op=MULT,
             )
-            nc.vector.tensor_tensor(
-                out=t2[:, :w].rearrange("p (h j c) -> p h j c", h=n, c=2),
-                in0=y[:, :w].rearrange("p (h j c) -> p h j c", h=n, c=2)[:, :, :, ::-1],
-                in1=sin_t[:, lt, :].rearrange("p (j c) -> p j c", c=2).unsqueeze(1).to_broadcast([P, n, HD // 2, 2]),
-                op=MULT,
-            )
+            parts = 2 if shared(i) else 1
+            n2 = n // parts
+            for a in range(parts):
+                cols = slice(a * n2 * HD, (a + 1) * n2 * HD)
+                nc.vector.tensor_tensor(
+                    out=t2[:, cols].rearrange("p (h j c) -> p h j c", h=n2, c=2),
+                    in0=y[:, cols].rearrange("p (h j c) -> p h j c", h=n2, c=2)[:, :, :, ::-1],
+                    in1=sin_t[:, lt, :].rearrange("p (j c) -> p j c", c=2).unsqueeze(1).to_broadcast([P, n2, HD // 2, 2]),
+                    op=MULT,
+                )
             ssm = work.tile([P, HPB], F32, name="ssm", bufs=4)
             nc.gpsimd.tensor_scalar(out=ssm[:, :n], in0=ss[:, :n], scalar1=1e-24, scalar2=None, op0=MAX)
             state[i] = (t1, t2, ssm)
 
         def shared(i):
             w = sum(units[i][3])
-            return w // 2 if w >= W // 2 else 0
+            return 3 * w // 8 if w >= W // 2 else 0
 
         def add_g(i):
             t1, t2, ssm = state[i]
@@ -245,7 +250,10 @@ def tile_tttwrapper_pb_kernel(
             nc.sync.dma_start(out=dst[m * P : (m + 1) * P, col : col + w], in_=o[:, :w])
 
         units = []
-        for s in range(2 * NB):
+        for c in (0, 512):
+            for m in range(MT):
+                units.append((0, m, c, [512]))
+        for s in range(1, 2 * NB):
             for m in range(MT):
                 left = (2 * NB - s) * MT - m
                 if left > 4:
@@ -262,8 +270,6 @@ def tile_tttwrapper_pb_kernel(
             s, m, c0, groups = units[i]
             if i == 0:
                 matmuls(0, [(0, 0, 512), (1, 0, 512)])
-                matmuls(0, [(0, 512, 512)])
-                matmuls(0, [(1, 512, 512)])
             elif i > 1:
                 at = c0
                 for gw in groups:
@@ -277,10 +283,6 @@ def tile_tttwrapper_pb_kernel(
             rotate(i)
             if i > 0:
                 finish(i - 1)
-            if i == 0:
-                nc.gpsimd.dma_start(out=bias_q[:], in_=wq_b[W:D].partition_broadcast(P))
-            if i == 5:
-                nc.gpsimd.dma_start(out=bias_u[:], in_=wu_b.partition_broadcast(P))
             if m == 0 and c0 == 0 and s >= 2 and s + RING - 1 < 2 * NB:
                 load_block(s + RING - 1)
         last = len(units) - 1

@@ -1,6 +1,7 @@
 from contextlib import ExitStack
 
 import concourse.mybir as mybir
+from concourse.masks import make_identity
 
 F32 = mybir.dt.float32
 BF16 = mybir.dt.bfloat16
@@ -22,6 +23,7 @@ W = 1024
 NB = D // W
 HPB = W // HD
 RING = 3
+LAG = 2
 
 FLOPS = 2 * TOK * D * (2 * D)
 
@@ -38,7 +40,8 @@ def tile_tttwrapper_pb_kernel(
     with ExitStack() as ctx:
         keep = ctx.enter_context(tc.tile_pool(name="keep", bufs=1))
         work = ctx.enter_context(tc.tile_pool(name="work", bufs=2))
-        psum = ctx.enter_context(tc.psum_pool(name="psum", bufs=8))
+        psum = ctx.enter_context(tc.psum_pool(name="psum", bufs=6))
+        tables = ctx.enter_context(tc.psum_pool(name="tables", bufs=1))
         ctx.enter_context(tc.manual_schedule())
 
         xc = keep.tile([P, G, 2 * TOK], U8, align_bytes=256, name="xc")
@@ -57,8 +60,11 @@ def tile_tttwrapper_pb_kernel(
             rs = keep.tile([P, G, W], U8, align_bytes=256, name="rs%d" % r)
             ring_c.append(rc)
             ring_s.append(rs)
-        cos_t = keep.tile([P, 2, HD], F32, name="cos_t")
-        sin_t = keep.tile([P, 2, HD], F32, name="sin_t")
+        cos_b = keep.tile([P, 2, HD], BF16, name="cos_b")
+        sin_b = keep.tile([P, 2, HD], BF16, name="sin_b")
+        cos_t = tables.tile([P, 2, HD], F32, name="cos_t")
+        sin_t = tables.tile([P, 2, HD], F32, name="sin_t")
+        ident = keep.tile([P, P], BF16, name="ident")
         fr = keep.tile([P, 2, HD], BF16, name="fr")
         ones = keep.tile([P, P], BF16, name="ones")
         brow = keep.tile([P, W], BF16, name="brow")
@@ -82,10 +88,11 @@ def tile_tttwrapper_pb_kernel(
             )
 
         nc.vector.memset(xs[:].rearrange("p g n -> p (g n)").bitcast(I32), 0)
-        nc.gpsimd.memset(brow[:], 0.0)
+        nc.gpsimd.memset(brow[:].bitcast(I32), 0)
         nc.gpsimd.dma_start(out=brow[0:1, :], in_=wq_b[0:W].unsqueeze(0))
         nc.gpsimd.dma_start(out=fr[:], in_=freqs.rearrange("(t p) j c -> p t (j c)", p=P))
-        nc.gpsimd.memset(ones[:], 1.0)
+        nc.vector.memset(ones[:], 1.0)
+        make_identity(nc, ident[:])
         nc.vector.memset(half_s[0][:].rearrange("p g n -> p (g n)").bitcast(I32), 0)
         nc.vector.memset(half_s[1][:].rearrange("p g n -> p (g n)").bitcast(I32), 0)
         nc.vector.memset(ring_s[0][:].rearrange("p g n -> p (g n)").bitcast(I32), 0)
@@ -122,8 +129,8 @@ def tile_tttwrapper_pb_kernel(
             nc.scalar.copy(out=bias0[:, h * (W // 2) : (h + 1) * (W // 2)], in_=bank[:])
 
         frv = fr[:].rearrange("p t (j c) -> p t j c", c=2)
-        cv = cos_t[:].rearrange("p t (j c) -> p t j c", c=2)
-        sv = sin_t[:].rearrange("p t (j c) -> p t j c", c=2)
+        cv = cos_b[:].rearrange("p t (j c) -> p t j c", c=2)
+        sv = sin_b[:].rearrange("p t (j c) -> p t j c", c=2)
         nc.vector.tensor_copy(out=cv[:, :, :, 0], in_=frv[:, :, :, 0])
         nc.vector.tensor_copy(out=cv[:, :, :, 1], in_=frv[:, :, :, 0])
         nc.vector.tensor_scalar_mul(out=sv[:, :, :, 0], in0=frv[:, :, :, 1], scalar1=-1.0)
@@ -138,22 +145,49 @@ def tile_tttwrapper_pb_kernel(
 
         banks = {}
 
+        def mx_pass(s, m, c, w, g):
+            wc, ws = weights(s, c, w, g)
+            nc.tensor.matmul_mx(
+                out=banks[(s, m, c)][:, :w],
+                lhsT=xc[:, g, 2 * P * m : 2 * P * (m + 1)].bitcast(FP4X4),
+                lhsT_scale=xs[:, g, P * m : P * (m + 1)],
+                rhs=wc.bitcast(FP4X4),
+                rhs_scale=ws,
+                start=(g == 0),
+                stop=(g == G - 1),
+            )
+
         def matmuls(s, members):
             for m, c, w in members:
                 bank = psum.tile([P, W // 2], F32, name="bank")
                 banks[(s, m, c)] = bank
             for g in range(G):
                 for m, c, w in members:
-                    wc, ws = weights(s, c, w, g)
-                    nc.tensor.matmul_mx(
-                        out=banks[(s, m, c)][:, :w],
-                        lhsT=xc[:, g, 2 * P * m : 2 * P * (m + 1)].bitcast(FP4X4),
-                        lhsT_scale=xs[:, g, P * m : P * (m + 1)],
-                        rhs=wc.bitcast(FP4X4),
-                        rhs_scale=ws,
-                        start=(g == 0),
-                        stop=(g == G - 1),
-                    )
+                    mx_pass(s, m, c, w, g)
+
+        def spread_tables():
+            for dst, src in ((cos_t, cos_b), (sin_t, sin_b)):
+                nc.tensor.matmul(
+                    out=dst[:].rearrange("p t f -> p (t f)"),
+                    lhsT=ident[:],
+                    rhs=src[:].rearrange("p t f -> p (t f)"),
+                    start=True,
+                    stop=True,
+                )
+
+        def first_matmuls():
+            pairs = [[(0, 0), (1, 0)], [(2, 0), (3, 0)]]
+            for pair in pairs:
+                for m, c in pair:
+                    bank = psum.tile([P, W // 2], F32, name="bank")
+                    banks[(0, m, c)] = bank
+            for k in range(G + LAG):
+                for pair, g in ((pairs[0], k), (pairs[1], k - LAG)):
+                    if 0 <= g < G:
+                        for m, c in pair:
+                            mx_pass(0, m, c, W // 2, g)
+                if k == 3:
+                    spread_tables()
 
         def bias_of(s):
             if s == 0:
@@ -198,23 +232,18 @@ def tile_tttwrapper_pb_kernel(
                 in1=cos_t[:, lt, :].unsqueeze(1).to_broadcast([P, n, HD]),
                 op=MULT,
             )
-            parts = 2 if shared(i) else 1
-            n2 = n // parts
-            for a in range(parts):
-                cols = slice(a * n2 * HD, (a + 1) * n2 * HD)
-                nc.vector.tensor_tensor(
-                    out=t2[:, cols].rearrange("p (h j c) -> p h j c", h=n2, c=2),
-                    in0=y[:, cols].rearrange("p (h j c) -> p h j c", h=n2, c=2)[:, :, :, ::-1],
-                    in1=sin_t[:, lt, :].rearrange("p (j c) -> p j c", c=2).unsqueeze(1).to_broadcast([P, n2, HD // 2, 2]),
-                    op=MULT,
-                )
+            nc.vector.tensor_tensor(
+                out=t2[:, :w].rearrange("p (h j c) -> p h j c", h=n, c=2),
+                in0=y[:, :w].rearrange("p (h j c) -> p h j c", h=n, c=2)[:, :, :, ::-1],
+                in1=sin_t[:, lt, :].rearrange("p (j c) -> p j c", c=2).unsqueeze(1).to_broadcast([P, n, HD // 2, 2]),
+                op=MULT,
+            )
             ssm = work.tile([P, HPB], F32, name="ssm", bufs=4)
             nc.gpsimd.tensor_scalar(out=ssm[:, :n], in0=ss[:, :n], scalar1=1e-24, scalar2=None, op0=MAX)
             state[i] = (t1, t2, ssm)
 
         def shared(i):
-            w = sum(units[i][3])
-            return 3 * w // 8 if w >= W // 2 else 0
+            return sum(units[i][3]) if i < len(units) - 1 else 0
 
         def add_g(i):
             t1, t2, ssm = state[i]
@@ -228,6 +257,8 @@ def tile_tttwrapper_pb_kernel(
             t1, t2, ssm, u = state[i]
             k = shared(i)
             w = sum(units[i][3])
+            if k == w:
+                return
             nc.vector.tensor_tensor(out=u[:, k:w], in0=t1[:, k:w], in1=t2[:, k:w], op=ADD)
 
         def finish(i):
@@ -269,8 +300,8 @@ def tile_tttwrapper_pb_kernel(
         for i in range(len(units)):
             s, m, c0, groups = units[i]
             if i == 0:
-                matmuls(0, [(0, 0, 512), (1, 0, 512)])
-            elif i > 1:
+                first_matmuls()
+            elif i > 3:
                 at = c0
                 for gw in groups:
                     matmuls(s, [(m, at, gw)])

from contextlib import ExitStack

import concourse.mybir as mybir
from concourse.masks import make_identity

F32 = mybir.dt.float32
BF16 = mybir.dt.bfloat16
I32 = mybir.dt.int32
U8 = mybir.dt.uint8
FP4X4 = mybir.dt.float4_e2m1fn_x4
ADD = mybir.AluOpType.add
MULT = mybir.AluOpType.mult
MAX = mybir.AluOpType.max
ACT = mybir.ActivationFunctionType

P = 128
TOK = 512
D = 4096
HD = 256
G = D // 512
MT = TOK // P
W = 1024
NB = D // W
HPB = W // HD
RING = 3
LAG = 2

FLOPS = 2 * TOK * D * (2 * D)


def tile_tttwrapper_pb_kernel(
    tc, x_words, x_scales, freqs, wq_words, wq_scales, wq_b, wu_words, wu_scales, wu_b, out_q, out_u
):
    nc = tc.nc
    streams = [
        (wq_words, wq_scales, wq_b, out_q.rearrange("b l h f -> (b l) (h f)")),
        (wu_words, wu_scales, wu_b, out_u.rearrange("b l h f -> (b l) (h f)")),
    ]

    with ExitStack() as ctx:
        keep = ctx.enter_context(tc.tile_pool(name="keep", bufs=1))
        work = ctx.enter_context(tc.tile_pool(name="work", bufs=2))
        psum = ctx.enter_context(tc.psum_pool(name="psum", bufs=6))
        tables = ctx.enter_context(tc.psum_pool(name="tables", bufs=1))
        ctx.enter_context(tc.manual_schedule())

        xc = keep.tile([P, G, 2 * TOK], U8, align_bytes=256, name="xc")
        xs = keep.tile([P, G, TOK], U8, align_bytes=256, name="xs")
        half_c = []
        half_s = []
        for h in range(2):
            hc = keep.tile([P, G, W], U8, align_bytes=256, name="hc%d" % h)
            hs = keep.tile([P, G, W // 2], U8, align_bytes=256, name="hs%d" % h)
            half_c.append(hc)
            half_s.append(hs)
        ring_c = []
        ring_s = []
        for r in range(RING):
            rc = keep.tile([P, G, 2 * W], U8, align_bytes=256, name="rc%d" % r)
            rs = keep.tile([P, G, W], U8, align_bytes=256, name="rs%d" % r)
            ring_c.append(rc)
            ring_s.append(rs)
        cos_b = keep.tile([P, 2, HD], BF16, name="cos_b")
        sin_b = keep.tile([P, 2, HD], BF16, name="sin_b")
        cos_t = tables.tile([P, 2, HD], F32, name="cos_t")
        sin_t = tables.tile([P, 2, HD], F32, name="sin_t")
        ident = keep.tile([P, P], BF16, name="ident")
        fr = keep.tile([P, 2, HD], BF16, name="fr")
        ones = keep.tile([P, P], BF16, name="ones")
        brow = keep.tile([P, W], BF16, name="brow")
        bias0 = keep.tile([P, W], F32, name="bias0")
        ring_b = []
        for r in range(RING):
            rb = keep.tile([P, W], BF16, name="rb%d" % r)
            ring_b.append(rb)

        def load_scales(dst, src, c0, width):
            for r in range(4):
                nc.sync.dma_start(
                    out=dst[r:P:32, :, :].bitcast(I32),
                    in_=src[:, r:16:4, c0 : c0 + width].rearrange("g q n -> q g n").bitcast(I32),
                )

        def load_codes(dst, src, g0, g1, c0, width):
            nc.sync.dma_start(
                out=dst[:, g0:g1, :].bitcast(I32),
                in_=src[g0:g1, :, 2 * c0 : 2 * (c0 + width)].rearrange("g p n -> p g n").bitcast(I32),
            )

        nc.vector.memset(xs[:].rearrange("p g n -> p (g n)").bitcast(I32), 0)
        nc.gpsimd.memset(brow[:].bitcast(I32), 0)
        nc.gpsimd.dma_start(out=brow[0:1, :], in_=wq_b[0:W].unsqueeze(0))
        nc.gpsimd.dma_start(out=fr[:], in_=freqs.rearrange("(t p) j c -> p t (j c)", p=P))
        nc.vector.memset(ones[:], 1.0)
        make_identity(nc, ident[:])
        nc.vector.memset(half_s[0][:].rearrange("p g n -> p (g n)").bitcast(I32), 0)
        nc.vector.memset(half_s[1][:].rearrange("p g n -> p (g n)").bitcast(I32), 0)
        nc.vector.memset(ring_s[0][:].rearrange("p g n -> p (g n)").bitcast(I32), 0)
        for r in range(1, RING):
            nc.gpsimd.memset(ring_s[r][:].rearrange("p g n -> p (g n)").bitcast(I32), 0)

        load_codes(xc, x_words, 0, 1, 0, TOK)
        load_codes(half_c[0], wq_words, 0, 1, 0, W // 2)
        load_scales(xs, x_scales, 0, TOK)
        load_scales(half_s[0], wq_scales, 0, W // 2)
        load_codes(xc, x_words, 1, 4, 0, TOK)
        load_codes(half_c[0], wq_words, 1, 4, 0, W // 2)
        load_codes(xc, x_words, 4, 8, 0, TOK)
        load_codes(half_c[0], wq_words, 4, 8, 0, W // 2)
        load_codes(half_c[1], wq_words, 0, 8, W // 2, W // 2)
        load_scales(half_s[1], wq_scales, W // 2, W // 2)

        def load_block(s):
            words, scales, bias, dst = streams[s // NB]
            c0 = (s % NB) * W
            r = (s - 1) % RING
            load_codes(ring_c[r], words, 0, G, c0, W)
            load_scales(ring_s[r], scales, c0, W)
            nc.sync.dma_start(out=ring_b[r][:], in_=bias[c0 : c0 + W].partition_broadcast(P))

        for s in range(1, 1 + RING):
            load_block(s)

        for h in range(2):
            bank = psum.tile([P, W // 2], F32, name="bank")
            nc.tensor.matmul(
                out=bank[:], lhsT=ones[:], rhs=brow[:, h * (W // 2) : (h + 1) * (W // 2)], start=True, stop=True
            )
            nc.scalar.copy(out=bias0[:, h * (W // 2) : (h + 1) * (W // 2)], in_=bank[:])

        frv = fr[:].rearrange("p t (j c) -> p t j c", c=2)
        cv = cos_b[:].rearrange("p t (j c) -> p t j c", c=2)
        sv = sin_b[:].rearrange("p t (j c) -> p t j c", c=2)
        nc.vector.tensor_copy(out=cv[:, :, :, 0], in_=frv[:, :, :, 0])
        nc.vector.tensor_copy(out=cv[:, :, :, 1], in_=frv[:, :, :, 0])
        nc.vector.tensor_scalar_mul(out=sv[:, :, :, 0], in0=frv[:, :, :, 1], scalar1=-1.0)
        nc.vector.tensor_copy(out=sv[:, :, :, 1], in_=frv[:, :, :, 1])

        def weights(s, c, w, g):
            if s == 0:
                h, c = divmod(c, W // 2)
                return half_c[h][:, g, 2 * c : 2 * (c + w)], half_s[h][:, g, c : c + w]
            r = (s - 1) % RING
            return ring_c[r][:, g, 2 * c : 2 * (c + w)], ring_s[r][:, g, c : c + w]

        banks = {}

        def mx_pass(s, m, c, w, g):
            wc, ws = weights(s, c, w, g)
            nc.tensor.matmul_mx(
                out=banks[(s, m, c)][:, :w],
                lhsT=xc[:, g, 2 * P * m : 2 * P * (m + 1)].bitcast(FP4X4),
                lhsT_scale=xs[:, g, P * m : P * (m + 1)],
                rhs=wc.bitcast(FP4X4),
                rhs_scale=ws,
                start=(g == 0),
                stop=(g == G - 1),
            )

        def matmuls(s, members):
            for m, c, w in members:
                bank = psum.tile([P, W // 2], F32, name="bank")
                banks[(s, m, c)] = bank
            for g in range(G):
                for m, c, w in members:
                    mx_pass(s, m, c, w, g)

        def spread_tables():
            for dst, src in ((cos_t, cos_b), (sin_t, sin_b)):
                nc.tensor.matmul(
                    out=dst[:].rearrange("p t f -> p (t f)"),
                    lhsT=ident[:],
                    rhs=src[:].rearrange("p t f -> p (t f)"),
                    start=True,
                    stop=True,
                )

        def first_matmuls():
            pairs = [[(0, 0), (1, 0)], [(2, 0), (3, 0)]]
            for pair in pairs:
                for m, c in pair:
                    bank = psum.tile([P, W // 2], F32, name="bank")
                    banks[(0, m, c)] = bank
            for k in range(G + LAG):
                for pair, g in ((pairs[0], k), (pairs[1], k - LAG)):
                    if 0 <= g < G:
                        for m, c in pair:
                            mx_pass(0, m, c, W // 2, g)
                if k == 3:
                    spread_tables()

        def bias_of(s):
            if s == 0:
                return bias0[:]
            return ring_b[(s - 1) % RING][:]

        state = {}

        def front(i):
            s, m, c0, groups = units[i]
            w = sum(groups)
            y = work.tile([P, W], F32, name="y")
            b = bias_of(s)
            at = 0
            for gw in groups:
                nc.vector.tensor_tensor(
                    out=y[:, at : at + gw],
                    in0=banks[(s, m, c0 + at)][:, :gw],
                    in1=b[:, c0 + at : c0 + at + gw],
                    op=ADD,
                )
                at += gw
            ss = work.tile([P, HPB], F32, name="ss", bufs=4)
            for j in range(w // HD):
                junk = work.tile([P, HD], F32, name="junk")
                nc.scalar.activation(
                    out=junk[:], in_=y[:, j * HD : (j + 1) * HD], func=ACT.Square, accum_out=ss[:, j : j + 1]
                )
            state[i] = (y, ss)

        def rotate(i):
            s, m, c0, groups = units[i]
            w = sum(groups)
            n = w // HD
            y, ss = state[i]
            lt = m % 2
            t1 = work.tile([P, W], F32, name="t1")
            t2 = work.tile([P, W], F32, name="t2")
            nc.vector.tensor_tensor(
                out=t1[:, :w].rearrange("p (h f) -> p h f", h=n),
                in0=y[:, :w].rearrange("p (h f) -> p h f", h=n),
                in1=cos_t[:, lt, :].unsqueeze(1).to_broadcast([P, n, HD]),
                op=MULT,
            )
            nc.vector.tensor_tensor(
                out=t2[:, :w].rearrange("p (h j c) -> p h j c", h=n, c=2),
                in0=y[:, :w].rearrange("p (h j c) -> p h j c", h=n, c=2)[:, :, :, ::-1],
                in1=sin_t[:, lt, :].rearrange("p (j c) -> p j c", c=2).unsqueeze(1).to_broadcast([P, n, HD // 2, 2]),
                op=MULT,
            )
            ssm = work.tile([P, HPB], F32, name="ssm", bufs=4)
            nc.gpsimd.tensor_scalar(out=ssm[:, :n], in0=ss[:, :n], scalar1=1e-24, scalar2=None, op0=MAX)
            state[i] = (t1, t2, ssm)

        def shared(i):
            return sum(units[i][3]) if i < len(units) - 1 else 0

        def add_g(i):
            t1, t2, ssm = state[i]
            u = work.tile([P, W], F32, name="u", bufs=3)
            k = shared(i)
            if k:
                nc.gpsimd.tensor_tensor(out=u[:, :k], in0=t1[:, :k], in1=t2[:, :k], op=ADD)
            state[i] = (t1, t2, ssm, u)

        def add_v(i):
            t1, t2, ssm, u = state[i]
            k = shared(i)
            w = sum(units[i][3])
            if k == w:
                return
            nc.vector.tensor_tensor(out=u[:, k:w], in0=t1[:, k:w], in1=t2[:, k:w], op=ADD)

        def finish(i):
            t1, t2, ssm, u = state[i]
            s, m, c0, groups = units[i]
            w = sum(groups)
            n = w // HD
            inv = work.tile([P, HPB], F32, name="inv", bufs=4)
            nc.scalar.activation(out=inv[:, :n], in_=ssm[:, :n], func=ACT.Abs_reciprocal_sqrt)
            o = work.tile([P, W], F32, name="o", bufs=4)
            for j in range(n):
                nc.scalar.activation(
                    out=o[:, j * HD : (j + 1) * HD],
                    in_=u[:, j * HD : (j + 1) * HD],
                    func=ACT.Copy,
                    scale=inv[:, j : j + 1],
                )
            dst = streams[s // NB][3]
            col = (s % NB) * W + c0
            nc.sync.dma_start(out=dst[m * P : (m + 1) * P, col : col + w], in_=o[:, :w])

        units = []
        for c in (0, 512):
            for m in range(MT):
                units.append((0, m, c, [512]))
        for s in range(1, 2 * NB):
            for m in range(MT):
                left = (2 * NB - s) * MT - m
                if left > 4:
                    units.append((s, m, 0, [512, 512]))
                elif left > 1:
                    units.append((s, m, 0, [512]))
                    units.append((s, m, 512, [512]))
                else:
                    units.append((s, m, 0, [512]))
                    units.append((s, m, 512, [256]))
                    units.append((s, m, 768, [256]))

        for i in range(len(units)):
            s, m, c0, groups = units[i]
            if i == 0:
                first_matmuls()
            elif i > 3:
                at = c0
                for gw in groups:
                    matmuls(s, [(m, at, gw)])
                    at += gw
            if i > 0:
                add_g(i - 1)
            front(i)
            if i > 0:
                add_v(i - 1)
            rotate(i)
            if i > 0:
                finish(i - 1)
            if m == 0 and c0 == 0 and s >= 2 and s + RING - 1 < 2 * NB:
                load_block(s + RING - 1)
        last = len(units) - 1
        add_g(last)
        add_v(last)
        finish(last)
